import numpy as np
import ml_dtypes


def mxq(x, axis, fmt="e4m3"):
    dtype, down = {"e4m3": (ml_dtypes.float8_e4m3fn, 7), "e5m2": (ml_dtypes.float8_e5m2, 14)}[fmt]
    v = np.moveaxis(np.asarray(x, np.float32).astype(ml_dtypes.bfloat16).astype(np.float64), axis, -1)
    blocks = v.reshape(v.shape[:-1] + (-1, 32))
    amax = np.abs(blocks).max(-1, keepdims=True)
    byte = np.maximum(np.where(amax > 0, np.frexp(amax)[1] - 1 + 127, 0) - down, 1)
    scale = np.exp2(byte - 127.0)
    codes = (blocks / scale).astype(np.float32).astype(dtype).astype(np.float64)
    return np.moveaxis((codes * scale).reshape(v.shape), -1, axis)


WIDE = False


def mx_kscale(k):
    if not WIDE:
        return np.ones(k)
    levels = np.array([10, -10, 5, -5, 0])
    if k % 512:
        return np.exp2(np.random.permutation(np.resize(levels, k // 32))).repeat(32)
    a = np.empty((k // 512, 16))
    for p in range(k // 512):
        a[p, :8] = np.random.permutation(np.resize(levels, 8))
        for g in range(8):
            far = levels[np.abs(levels - a[p, g]) >= 10]
            a[p, g + 8] = far[np.random.randint(len(far))]
    return np.exp2(a.ravel()).repeat(32)


BF16 = ml_dtypes.bfloat16


def bf(x):
    return np.asarray(x, np.float32).astype(BF16)


def f64(x):
    return np.asarray(x).astype(np.float64)


B, L, A, W = 128, 512, 1024, 32
EPS = 1e-8


def sigmoid(v):
    return 1.0 / (1.0 + np.exp(-v))


def setup_inputs():
    s, t = mx_kscale(L), mx_kscale(A)
    return {
        "z_current": bf(np.random.standard_normal((B, L)) * s),
        "z_window": bf(np.random.standard_normal((W, B, L)) * s),
        "Wq": bf(np.random.standard_normal((A, L)) / np.sqrt(L) / s),
        "Wk": bf(np.random.standard_normal((A, L)) / np.sqrt(L) / s),
        "Wv": bf(np.random.standard_normal((A, L)) / np.sqrt(L) / s * t[:, None]),
        "Wo": bf(np.random.standard_normal((L, A)) * 2.0 / np.sqrt(A) / t),
    }


def reference(z_current, z_window, Wq, Wk, Wv, Wo):
    sig_q = sigmoid(mxq(f64(z_current), 1, "e4m3") @ mxq(f64(Wq), 1, "e4m3").T)
    zw = mxq(f64(z_window), 2, "e4m3")
    k = zw @ mxq(f64(Wk), 1, "e4m3").T
    v = zw @ mxq(f64(Wv), 1, "e4m3").T
    m = k.max(axis=(1, 2), keepdims=True)
    e = np.exp(k - m)
    num = (e * v).sum(0)
    den = EPS + e.sum(0)
    h = sig_q * (num / den)
    return mxq(h, 1, "e4m3") @ mxq(f64(Wo), 1, "e4m3").T

@@ -1,0 +1,353 @@
+from contextlib import ExitStack
+
+import concourse.mybir as mybir
+from concourse.masks import make_identity
+
+F32 = mybir.dt.float32
+BF16 = mybir.dt.bfloat16
+U32 = mybir.dt.uint32
+U8 = mybir.dt.uint8
+FP8X4 = mybir.dt.float8_e4m3fn_x4
+ACT = mybir.ActivationFunctionType
+ALU = mybir.AluOpType
+AXIS = mybir.AxisListType
+
+P = 128
+B, L, A, STEPS = 128, 512, 1024, 32
+EPS = 1e-8
+PACK = 4
+BANK = 512
+HALVES = A // BANK
+CHUNKS = A // P
+GROUP = 4
+LAG = 3
+
+FLOPS = 2 * B * L * A + 2 * 2 * STEPS * B * L * A + 2 * B * A * L
+
+
+def turn_pair(nc, bank, ident, pair, grouped_words):
+    for r, words in enumerate(pair):
+        for u in range(2):
+            nc.tensor.transpose(
+                out=bank[:, (2 * r + u) * P : (2 * r + u + 1) * P],
+                in_=words[:, u : 2 * P : 2],
+                identity=ident[:],
+            )
+    width = len(pair) * 2 * P
+    nc.scalar.copy(
+        out=grouped_words[:, 0:width].rearrange("p (r c u) -> p r c u", c=P, u=2),
+        in_=bank[:, 0:width].rearrange("p (r u c) -> p r c u", u=2, c=P),
+    )
+
+
+def tile_aftblock_pa_t_kernel(tc, z_current, z_window, Wq, Wk, Wv, Wo, out):
+    nc = tc.nc
+    with ExitStack() as ctx:
+        const = ctx.enter_context(tc.tile_pool(name="const", bufs=1))
+        raw = ctx.enter_context(tc.tile_pool(name="raw", bufs=1))
+        stage = ctx.enter_context(tc.tile_pool(name="stage", bufs=4))
+        quant = ctx.enter_context(tc.tile_pool(name="quant", bufs=1))
+        small = ctx.enter_context(tc.tile_pool(name="small", bufs=4))
+        e_pool = ctx.enter_context(tc.tile_pool(name="e_pool", bufs=LAG + 4))
+        prod_pool = ctx.enter_context(tc.tile_pool(name="prod_pool", bufs=3))
+        tail = ctx.enter_context(tc.tile_pool(name="tail", bufs=1))
+        sum_banks = ctx.enter_context(tc.psum_pool(name="sum_banks", bufs=1))
+        key_banks = ctx.enter_context(tc.psum_pool(name="key_banks", bufs=2))
+        value_banks = ctx.enter_context(tc.psum_pool(name="value_banks", bufs=2))
+        single_banks = ctx.enter_context(tc.psum_pool(name="single_banks", bufs=1))
+
+        ident = const.tile([P, P], F32, name="ident")
+        make_identity(nc, ident[:])
+        den = const.tile([P, A], F32, name="den")
+        nc.vector.memset(den[:], EPS)
+
+        ctx.enter_context(tc.manual_schedule())
+
+        wk_raw = raw.tile([P, HALVES, PACK * L], BF16, name="wk_raw")
+        wv_raw = raw.tile([P, HALVES, PACK * L], BF16, name="wv_raw")
+        wq_raw = raw.tile([P, HALVES, PACK * L], BF16, name="wq_raw")
+        wo_raw = raw.tile([P, L // P, A], BF16, name="wo_raw")
+        zc_raw = raw.tile([P, L], BF16, name="zc_raw")
+        z_raw = [raw.tile([P, GROUP, L], BF16, name="z_raw%d" % n) for n in range(STEPS // GROUP)]
+
+        def load_weight(tile_ap, weight, g):
+            nc.sync.dma_start(
+                out=tile_ap[:, g, :],
+                in_=weight.rearrange("(g j t) l -> j g (t l)", g=HALVES, t=PACK)[:, g, :],
+            )
+
+        def load_steps(n):
+            nc.sync.dma_start(
+                out=z_raw[n][:],
+                in_=z_window[n * GROUP : (n + 1) * GROUP].rearrange("w b l -> b w l"),
+            )
+
+        load_weight(wk_raw, Wk, 0)
+        load_steps(0)
+        load_weight(wk_raw, Wk, 1)
+        load_weight(wv_raw, Wv, 0)
+        load_steps(1)
+        load_weight(wv_raw, Wv, 1)
+        for n in range(2, STEPS // GROUP):
+            load_steps(n)
+        load_weight(wq_raw, Wq, 0)
+        load_weight(wq_raw, Wq, 1)
+        nc.sync.dma_start(out=zc_raw[:], in_=z_current)
+        nc.sync.dma_start(out=wo_raw[:], in_=Wo.rearrange("(c p) a -> p c a", p=P))
+
+        z_codes = quant.tile([P, STEPS * B], U32, name="z_codes", align_bytes=64)
+        z_scales = quant.tile([P, STEPS * B], U8, name="z_scales", align_bytes=64)
+        zc_codes = quant.tile([P, B], U32, name="zc_codes", align_bytes=64)
+        zc_scales = quant.tile([P, B], U8, name="zc_scales", align_bytes=64)
+        wk_codes = quant.tile([P, A], U32, name="wk_codes", align_bytes=64)
+        wk_scales = quant.tile([P, A], U8, name="wk_scales", align_bytes=64)
+        wv_codes = quant.tile([P, A], U32, name="wv_codes", align_bytes=64)
+        wv_scales = quant.tile([P, A], U8, name="wv_scales", align_bytes=64)
+        wq_codes = quant.tile([P, A], U32, name="wq_codes", align_bytes=64)
+        wq_scales = quant.tile([P, A], U8, name="wq_scales", align_bytes=64)
+        wo_codes = quant.tile([P, 2 * L], U32, name="wo_codes", align_bytes=64)
+        wo_scales = quant.tile([P, 2 * L], U8, name="wo_scales", align_bytes=64)
+
+        def weight_group(raw_tile, codes, scales, g):
+            words = raw_tile[:].bitcast(F32)
+            rows = [words[:, g, t * (L // 2) : (t + 1) * (L // 2)] for t in range(PACK)]
+            cols = slice(g * BANK, (g + 1) * BANK)
+            return (rows, codes[:, cols], scales[:, cols])
+
+        def steps_group(n):
+            words = z_raw[n][:].bitcast(F32)
+            cols = slice(n * GROUP * B, (n + 1) * GROUP * B)
+            return ([words[:, s, :] for s in range(GROUP)], z_codes[:, cols], z_scales[:, cols])
+
+        def output_weight_group(g):
+            words = wo_raw[:].bitcast(F32)
+            rows = [words[:, c, g * (BANK // 2) : (g + 1) * (BANK // 2)] for c in range(L // P)]
+            cols = slice(g * L, (g + 1) * L)
+            return (rows, wo_codes[:, cols], wo_scales[:, cols])
+
+        def new_grouped():
+            grouped = stage.tile([P, GROUP * P * PACK], BF16, tag="grouped", align_bytes=64)
+            return grouped
+
+        def turn_half(group, grouped, half, banks, tag):
+            bank = banks.tile([P, BANK], F32, tag=tag, name="turned")
+            words = grouped[:].bitcast(F32)[:, half * BANK : (half + 1) * BANK]
+            turn_pair(nc, bank, ident, group[0][2 * half : 2 * half + 2], words)
+
+        def quantise(group, grouped):
+            nc.vector.quantize_mx(
+                out=group[1].bitcast(FP8X4),
+                scales=group[2],
+                in_=grouped[:, 0 : len(group[0]) * P * PACK],
+            )
+
+        def turn_whole(group):
+            grouped = new_grouped()
+            for half in range(2):
+                turn_half(group, grouped, half, value_banks, "values")
+            return grouped
+
+        for group in [
+            weight_group(wk_raw, wk_codes, wk_scales, 0),
+            steps_group(0),
+            weight_group(wk_raw, wk_codes, wk_scales, 1),
+        ]:
+            quantise(group, turn_whole(group))
+        value_groups = [weight_group(wv_raw, wv_codes, wv_scales, g) for g in range(2)]
+        later_groups = [steps_group(n) for n in range(1, STEPS // GROUP)]
+        later_groups.extend([weight_group(wq_raw, wq_codes, wq_scales, g) for g in range(2)])
+        later_groups.append(([zc_raw[:].bitcast(F32)], zc_codes[:], zc_scales[:]))
+        later_groups.extend([output_weight_group(g) for g in range(2)])
+        stream = []
+        for index, group in enumerate(later_groups):
+            halves = (len(group[0]) + 1) // 2
+            stream.extend([(index, half, half == halves - 1) for half in range(halves)])
+
+        num_t = [sum_banks.tile([P, BANK], F32, name="num_t%d" % g) for g in range(HALVES)]
+
+        k_banks, v_banks, maxima, spreads, neg_maxes, e_tiles, prod_tiles = {}, {}, {}, {}, {}, {}, {}
+
+        def step_matmul(banks, tag, w, codes, scales):
+            step = slice(w * B, (w + 1) * B)
+            made = []
+            for h in range(HALVES):
+                cols = slice(h * BANK, (h + 1) * BANK)
+                bank = banks.tile([P, BANK], F32, tag=tag, name="bank_" + tag)
+                nc.tensor.matmul_mx(
+                    out=bank[:],
+                    lhsT=z_codes[:, step].bitcast(FP8X4),
+                    lhsT_scale=z_scales[:, step],
+                    rhs=codes[:, cols].bitcast(FP8X4),
+                    rhs_scale=scales[:, cols],
+                    start=True,
+                    stop=True,
+                )
+                made.append(bank)
+            return made
+
+        def park_keys(w, h):
+            if h == 0:
+                e_tiles[w] = e_pool.tile([P, A], F32, tag="e", name="e")
+                maxima[w] = small.tile([P, HALVES], F32, tag="maxima", name="maxima")
+            nc.vector.tensor_scalar(
+                out=e_tiles[w][:, h * BANK : (h + 1) * BANK],
+                in0=k_banks[w][h][:],
+                scalar1=1.0,
+                scalar2=(None if h == 0 else maxima[w][:, h - 1 : h]),
+                op0=ALU.mult,
+                op1=ALU.max,
+                accum_out=maxima[w][:, h : h + 1],
+            )
+
+        def spread_maxima(w):
+            spread = single_banks.tile([P, BANK], F32, tag="spread")
+            nc.tensor.transpose(
+                out=spread[:, 0:P],
+                in_=maxima[w][:, HALVES - 1 : HALVES].to_broadcast([P, P]),
+                identity=ident[:],
+            )
+            spreads[w] = spread
+
+        def step_maximum(w):
+            neg_max = small.tile([P, 1], F32, tag="neg_max")
+            nc.vector.tensor_reduce(
+                out=neg_max[:], in_=spreads[w][:, 0:P], axis=AXIS.X, op=ALU.max, negate=True
+            )
+            neg_maxes[w] = neg_max
+
+        def exponentials(w):
+            e = e_tiles[w]
+            nc.scalar.activation(
+                out=e[:], in_=e[:], func=ACT.Exp, bias=neg_maxes[w][:, 0:1], scale=1.0
+            )
+            if w < STEPS - 1:
+                nc.gpsimd.tensor_tensor(out=den[:], in0=den[:], in1=e[:], op=ALU.add)
+
+        def products(w):
+            prod = prod_pool.tile([P, A], F32, tag="prod")
+            for h in range(HALVES):
+                cols = slice(h * BANK, (h + 1) * BANK)
+                nc.vector.tensor_tensor(
+                    out=prod[:, cols], in0=v_banks[w][h][:], in1=e_tiles[w][:, cols], op=ALU.mult
+                )
+            prod_tiles[w] = prod
+
+        def add_transposed(bank, source, g, first, last):
+            for t in range(PACK):
+                c = g * PACK + t
+                nc.tensor.matmul(
+                    out=bank[:, t * B : (t + 1) * B],
+                    lhsT=source[:, c * P : (c + 1) * P],
+                    rhs=ident[:],
+                    is_transpose=True,
+                    start=(first and t == 0),
+                    stop=(last and t == PACK - 1),
+                )
+
+        def sum_products(w):
+            for g in range(HALVES):
+                add_transposed(num_t[g], prod_tiles[w], g, w == 0, w == STEPS - 1)
+
+        gate_t = tail.tile([P, A], F32, name="gate_t")
+        rec_t = tail.tile([P, A], F32, name="rec_t")
+        scale_t = tail.tile([P, A], F32, name="scale_t")
+
+        def gate():
+            for g in range(HALVES):
+                q_t = single_banks.tile([P, BANK], F32, tag=("turn", "spread")[g], name="q_t")
+                for t in range(PACK):
+                    c = g * PACK + t
+                    nc.tensor.matmul_mx(
+                        out=q_t[:, t * B : (t + 1) * B],
+                        lhsT=wq_codes[:, c * P : (c + 1) * P].bitcast(FP8X4),
+                        lhsT_scale=wq_scales[:, c * P : (c + 1) * P],
+                        rhs=zc_codes[:].bitcast(FP8X4),
+                        rhs_scale=zc_scales[:],
+                        start=True,
+                        stop=True,
+                    )
+                nc.scalar.activation(
+                    out=gate_t[:, g * BANK : (g + 1) * BANK], in_=q_t[:], func=ACT.Sigmoid
+                )
+
+        den_t = {}
+
+        def turn_denominator():
+            for g in range(HALVES):
+                den_t[g] = key_banks.tile([P, BANK], F32, tag="keys", name="den_t")
+                add_transposed(den_t[g], den, g, True, False)
+                add_transposed(den_t[g], e_tiles[STEPS - 1], g, False, True)
+
+        def gate_over_denominator():
+            for g in range(HALVES):
+                cols = slice(g * BANK, (g + 1) * BANK)
+                nc.vector.reciprocal(out=rec_t[:, cols], in_=den_t[g][:])
+                nc.vector.tensor_tensor(
+                    out=scale_t[:, cols], in0=rec_t[:, cols], in1=gate_t[:, cols], op=ALU.mult
+                )
+
+        value_grouped, later_grouped = {}, {}
+        for n in range(STEPS + LAG + 1):
+            j = n - LAG
+            if 2 <= n < STEPS + 2:
+                exponentials(n - 2)
+            if n < STEPS:
+                k_banks[n] = step_matmul(key_banks, "keys", n, wk_codes, wk_scales)
+            if n == STEPS + 1:
+                gate()
+            if 0 <= j < STEPS:
+                v_banks[j] = step_matmul(value_banks, "values", j, wv_codes, wv_scales)
+            if n < STEPS:
+                park_keys(n, 0)
+            if 1 <= n <= len(value_groups):
+                quantise(value_groups[n - 1], value_grouped[n - 1])
+            if 1 <= n <= len(stream) and stream[n - 1][2]:
+                quantise(later_groups[stream[n - 1][0]], later_grouped[stream[n - 1][0]])
+            if n < STEPS:
+                park_keys(n, 1)
+            if 1 <= n < STEPS + 1:
+                spread_maxima(n - 1)
+            if n == STEPS + 2:
+                turn_denominator()
+            if n < len(value_groups):
+                value_grouped[n] = turn_whole(value_groups[n])
+            if n < len(stream):
+                index, half = stream[n][0], stream[n][1]
+                if half == 0:
+                    later_grouped[index] = new_grouped()
+                turn_half(later_groups[index], later_grouped[index], half, single_banks, "turn")
+            if 1 <= j < STEPS + 1:
+                sum_products(j - 1)
+            if 0 <= j < STEPS:
+                products(j)
+            if 1 <= n < STEPS + 1:
+                step_maximum(n - 1)
+            if n == STEPS + 2:
+                gate_over_denominator()
+
+        h_grouped = tail.tile([P, HALVES * B * PACK], BF16, name="h_grouped", align_bytes=64)
+        h_codes = tail.tile([P, HALVES * B], U32, name="h_codes", align_bytes=64)
+        h_scales = tail.tile([P, HALVES * B], U8, name="h_scales", align_bytes=64)
+        for g in range(HALVES):
+            cols = slice(g * BANK, (g + 1) * BANK)
+            nc.vector.tensor_tensor(
+                out=h_grouped[:, cols].rearrange("p (b t) -> p b t", t=PACK),
+                in0=num_t[g][:].rearrange("p (t b) -> p b t", t=PACK),
+                in1=scale_t[:, cols].rearrange("p (t b) -> p b t", t=PACK),
+                op=ALU.mult,
+            )
+        nc.vector.quantize_mx(out=h_codes[:].bitcast(FP8X4), scales=h_scales[:], in_=h_grouped[:])
+        out_bank = single_banks.tile([P, BANK], F32, tag="turn")
+        for g in range(HALVES):
+            nc.tensor.matmul_mx(
+                out=out_bank[:],
+                lhsT=h_codes[:, g * B : (g + 1) * B].bitcast(FP8X4),
+                lhsT_scale=h_scales[:, g * B : (g + 1) * B],
+                rhs=wo_codes[:, g * L : (g + 1) * L].bitcast(FP8X4),
+                rhs_scale=wo_scales[:, g * L : (g + 1) * L],
+                start=(g == 0),
+                stop=(g == HALVES - 1),
+            )
+        result = tail.tile([P, L], F32, name="result")
+        nc.scalar.copy(out=result[:], in_=out_bank[:])
+        nc.sync.dma_start(out=out, in_=result[:])

@@ -18,23 +18,41 @@ EPS = 1e-8
 PACK = 4
 BANK = 512
 HALVES = A // BANK
-CHUNKS = A // P
 GROUP = 4
-LAG = 3
+LAG = 6
+PE_ADDS = 3
+QUADS = (2, 2, 4, 4, 4, 4, 4, 4, 2, 2)
+AHEAD = 2
+SPLIT_FROM = 20
+WARM = 6
+HEADWARM = 0
+GATE_AT = (19, 23)
 
 FLOPS = 2 * B * L * A + 2 * 2 * STEPS * B * L * A + 2 * B * A * L
 
 
-def turn_pair(nc, bank, ident, pair, grouped_words):
+def order_pair(nc, pair, ordered):
+    for r, words in enumerate(pair):
+        nc.scalar.copy(
+            out=ordered[:, r * 2 * P : (r + 1) * 2 * P].rearrange("p (u c) -> p u c", u=2),
+            in_=words.rearrange("p (c u) -> p u c", u=2),
+        )
+
+
+def turn_pair(nc, copy, bank, ident, pair, ordered, grouped_words):
     for r, words in enumerate(pair):
         for u in range(2):
+            if ordered is None:
+                source = words[:, u : 2 * P : 2]
+            else:
+                source = ordered[:, (2 * r + u) * P : (2 * r + u + 1) * P]
             nc.tensor.transpose(
                 out=bank[:, (2 * r + u) * P : (2 * r + u + 1) * P],
-                in_=words[:, u : 2 * P : 2],
+                in_=source,
                 identity=ident[:],
             )
     width = len(pair) * 2 * P
-    nc.scalar.copy(
+    copy(
         out=grouped_words[:, 0:width].rearrange("p (r c u) -> p r c u", c=P, u=2),
         in_=bank[:, 0:width].rearrange("p (r u c) -> p r c u", u=2, c=P),
     )
@@ -46,6 +64,7 @@ def tile_aftblock_pa_t_kernel(tc, z_current, z_window, Wq, Wk, Wv, Wo, out):
         const = ctx.enter_context(tc.tile_pool(name="const", bufs=1))
         raw = ctx.enter_context(tc.tile_pool(name="raw", bufs=1))
         stage = ctx.enter_context(tc.tile_pool(name="stage", bufs=4))
+        order_pool = ctx.enter_context(tc.tile_pool(name="order_pool", bufs=4))
         quant = ctx.enter_context(tc.tile_pool(name="quant", bufs=1))
         small = ctx.enter_context(tc.tile_pool(name="small", bufs=4))
         e_pool = ctx.enter_context(tc.tile_pool(name="e_pool", bufs=LAG + 4))
@@ -60,8 +79,16 @@ def tile_aftblock_pa_t_kernel(tc, z_current, z_window, Wq, Wk, Wv, Wo, out):
         make_identity(nc, ident[:])
         den = const.tile([P, A], F32, name="den")
         nc.vector.memset(den[:], EPS)
+        row_maxima = [const.tile([P, P], F32, name="row_maxima%d" % i) for i in range(2)]
+        for tile_of_maxima in row_maxima:
+            nc.vector.memset(tile_of_maxima[:], 0.0)
+        warm = const.tile([P, 1], F32, name="warm")
+        nc.vector.memset(warm[:], 1.0)
+        cold = const.tile([P, BANK], BF16, name="cold")
+        nc.gpsimd.memset(cold[:], 0.0)
 
         ctx.enter_context(tc.manual_schedule())
+        nc.scalar.activation(out=warm[:], in_=warm[:], func=ACT.Exp)
 
         wk_raw = raw.tile([P, HALVES, PACK * L], BF16, name="wk_raw")
         wv_raw = raw.tile([P, HALVES, PACK * L], BF16, name="wv_raw")
@@ -70,28 +97,33 @@ def tile_aftblock_pa_t_kernel(tc, z_current, z_window, Wq, Wk, Wv, Wo, out):
         zc_raw = raw.tile([P, L], BF16, name="zc_raw")
         z_raw = [raw.tile([P, GROUP, L], BF16, name="z_raw%d" % n) for n in range(STEPS // GROUP)]
 
-        def load_weight(tile_ap, weight, g):
+        def load_weight(tile_ap, weight, g, cols):
             nc.sync.dma_start(
-                out=tile_ap[:, g, :],
-                in_=weight.rearrange("(g j t) l -> j g (t l)", g=HALVES, t=PACK)[:, g, :],
+                out=tile_ap[:, g, cols],
+                in_=weight.rearrange("(g j t) l -> j g (t l)", g=HALVES, t=PACK)[:, g, cols],
             )
 
-        def load_steps(n):
+        def load_steps(n, first, last):
             nc.sync.dma_start(
-                out=z_raw[n][:],
-                in_=z_window[n * GROUP : (n + 1) * GROUP].rearrange("w b l -> b w l"),
+                out=z_raw[n][:, first:last, :],
+                in_=z_window[n * GROUP + first : n * GROUP + last].rearrange("w b l -> b w l"),
             )
 
-        load_weight(wk_raw, Wk, 0)
-        load_steps(0)
-        load_weight(wk_raw, Wk, 1)
-        load_weight(wv_raw, Wv, 0)
-        load_steps(1)
-        load_weight(wv_raw, Wv, 1)
+        whole = slice(0, PACK * L)
+        halves = (slice(0, 2 * L), slice(2 * L, 4 * L))
+        load_weight(wk_raw, Wk, 0, halves[0])
+        load_weight(wk_raw, Wk, 0, halves[1])
+        load_steps(0, 0, 2)
+        load_weight(wk_raw, Wk, 1, halves[0])
+        load_weight(wk_raw, Wk, 1, halves[1])
+        load_steps(0, 2, 4)
+        load_weight(wv_raw, Wv, 0, whole)
+        load_steps(1, 0, 4)
+        load_weight(wv_raw, Wv, 1, whole)
         for n in range(2, STEPS // GROUP):
-            load_steps(n)
-        load_weight(wq_raw, Wq, 0)
-        load_weight(wq_raw, Wq, 1)
+            load_steps(n, 0, 4)
+        load_weight(wq_raw, Wq, 0, whole)
+        load_weight(wq_raw, Wq, 1, whole)
         nc.sync.dma_start(out=zc_raw[:], in_=z_current)
         nc.sync.dma_start(out=wo_raw[:], in_=Wo.rearrange("(c p) a -> p c a", p=P))
 
@@ -125,14 +157,23 @@ def tile_aftblock_pa_t_kernel(tc, z_current, z_window, Wq, Wk, Wv, Wo, out):
             cols = slice(g * L, (g + 1) * L)
             return (rows, wo_codes[:, cols], wo_scales[:, cols])
 
+        def half_group(group, half):
+            cols = slice(2 * half * P, 2 * (half + 1) * P)
+            return (group[0][2 * half : 2 * half + 2], group[1][:, cols], group[2][:, cols])
+
         def new_grouped():
             grouped = stage.tile([P, GROUP * P * PACK], BF16, tag="grouped", align_bytes=64)
             return grouped
 
-        def turn_half(group, grouped, half, banks, tag):
+        def order_half(group, half):
+            ordered = order_pool.tile([P, BANK], F32, tag="ordered", name="ordered")
+            order_pair(nc, group[0][2 * half : 2 * half + 2], ordered)
+            return ordered
+
+        def turn_half(copy, group, grouped, half, banks, tag, ordered=None):
             bank = banks.tile([P, BANK], F32, tag=tag, name="turned")
             words = grouped[:].bitcast(F32)[:, half * BANK : (half + 1) * BANK]
-            turn_pair(nc, bank, ident, group[0][2 * half : 2 * half + 2], words)
+            turn_pair(nc, copy, bank, ident, group[0][2 * half : 2 * half + 2], ordered, words)
 
         def quantise(group, grouped):
             nc.vector.quantize_mx(
@@ -141,31 +182,59 @@ def tile_aftblock_pa_t_kernel(tc, z_current, z_window, Wq, Wk, Wv, Wo, out):
                 in_=grouped[:, 0 : len(group[0]) * P * PACK],
             )
 
-        def turn_whole(group):
-            grouped = new_grouped()
-            for half in range(2):
-                turn_half(group, grouped, half, value_banks, "values")
-            return grouped
-
-        for group in [
-            weight_group(wk_raw, wk_codes, wk_scales, 0),
-            steps_group(0),
-            weight_group(wk_raw, wk_codes, wk_scales, 1),
-        ]:
-            quantise(group, turn_whole(group))
-        value_groups = [weight_group(wv_raw, wv_codes, wv_scales, g) for g in range(2)]
-        later_groups = [steps_group(n) for n in range(1, STEPS // GROUP)]
-        later_groups.extend([weight_group(wq_raw, wq_codes, wq_scales, g) for g in range(2)])
-        later_groups.append(([zc_raw[:].bitcast(F32)], zc_codes[:], zc_scales[:]))
-        later_groups.extend([output_weight_group(g) for g in range(2)])
-        stream = []
-        for index, group in enumerate(later_groups):
-            halves = (len(group[0]) + 1) // 2
-            stream.extend([(index, half, half == halves - 1) for half in range(halves)])
-
         num_t = [sum_banks.tile([P, BANK], F32, name="num_t%d" % g) for g in range(HALVES)]
 
-        k_banks, v_banks, maxima, spreads, neg_maxes, e_tiles, prod_tiles = {}, {}, {}, {}, {}, {}, {}
+        def keep_warm(count):
+            for i in range(count):
+                nc.tensor.matmul(
+                    out=num_t[0][:], lhsT=cold[:, 0:P], rhs=cold[:], start=True, stop=True
+                )
+
+        keep_warm(WARM)
+        steps_groups = [steps_group(n) for n in range(STEPS // GROUP)]
+        key_weights = [weight_group(wk_raw, wk_codes, wk_scales, g) for g in range(2)]
+        head = [
+            (half_group(key_weights[0], 0), nc.scalar.copy, value_banks, "values"),
+            (half_group(key_weights[0], 1), nc.vector.tensor_copy, value_banks, "values"),
+            (half_group(steps_groups[0], 0), nc.scalar.copy, single_banks, "turn"),
+            (half_group(key_weights[1], 0), nc.vector.tensor_copy, single_banks, "spread"),
+            (half_group(key_weights[1], 1), nc.scalar.copy, value_banks, "values"),
+        ]
+        pending = []
+        for group, copy, banks, tag in head:
+            grouped = new_grouped()
+            turn_half(copy, group, grouped, 0, banks, tag)
+            keep_warm(HEADWARM)
+            pending.append((group, grouped))
+            if len(pending) > 1:
+                quantise(*pending.pop(0))
+        quantise(*pending.pop(0))
+        value_weights = [weight_group(wv_raw, wv_codes, wv_scales, g) for g in range(2)]
+        tail_groups = [weight_group(wq_raw, wq_codes, wq_scales, g) for g in range(2)]
+        tail_groups.append(([zc_raw[:].bitcast(F32)], zc_codes[:], zc_scales[:]))
+        tail_groups.extend([output_weight_group(g) for g in range(2)])
+        later_groups = [half_group(steps_groups[0], 1)] + steps_groups[1:3]
+        for i in range(5):
+            later_groups.append(steps_groups[3 + i])
+            later_groups.append(tail_groups[i])
+        stream = []
+        for index, group in enumerate(later_groups):
+            pairs = (len(group[0]) + 1) // 2
+            stream.extend([(index, half, half == pairs - 1) for half in range(pairs)])
+        value_stream = [(g, half) for g in range(2) for half in range(2)]
+
+        k_banks, v_banks, first_half_max, turned_max, quad_max, spread_max = {}, {}, {}, {}, {}, {}
+        neg_maxes, e_tiles, prod_tiles = {}, {}, {}
+
+        quad_of, quad_end, exp_steps, exp_iteration = {}, {}, {}, {}
+        first = 0
+        for quad, size in enumerate(QUADS):
+            for i in range(size):
+                quad_of[first + i] = (quad, i)
+                exp_iteration[first + i] = first + size + 1 + i
+                exp_steps.setdefault(first + size + 1 + i, []).append(first + i)
+            quad_end[first + size - 1] = quad
+            first += size
 
         def step_matmul(banks, tag, w, codes, scales):
             step = slice(w * B, (w + 1) * B)
@@ -188,49 +257,79 @@ def tile_aftblock_pa_t_kernel(tc, z_current, z_window, Wq, Wk, Wv, Wo, out):
         def park_keys(w, h):
             if h == 0:
                 e_tiles[w] = e_pool.tile([P, A], F32, tag="e", name="e")
-                maxima[w] = small.tile([P, HALVES], F32, tag="maxima", name="maxima")
+                first_half_max[w] = small.tile([P, 1], F32, tag="first_half_max", name="first_half")
+                accumulator = first_half_max[w][:, 0:1]
+            else:
+                quad, column = quad_of[w]
+                accumulator = row_maxima[quad % 2][:, column : column + 1]
             nc.vector.tensor_scalar(
                 out=e_tiles[w][:, h * BANK : (h + 1) * BANK],
                 in0=k_banks[w][h][:],
                 scalar1=1.0,
-                scalar2=(None if h == 0 else maxima[w][:, h - 1 : h]),
+                scalar2=(None if h == 0 else first_half_max[w][:, 0:1]),
                 op0=ALU.mult,
                 op1=ALU.max,
-                accum_out=maxima[w][:, h : h + 1],
+                accum_out=accumulator,
             )
 
-        def spread_maxima(w):
-            spread = single_banks.tile([P, BANK], F32, tag="spread")
+        def turn_maxima(quad):
+            turned = single_banks.tile([P, BANK], F32, tag="spread", name="turned_max")
+            nc.tensor.transpose(out=turned[:, 0:P], in_=row_maxima[quad % 2][:], identity=ident[:])
+            turned_max[quad] = turned
+
+        def reduce_maxima(quad):
+            neg = small.tile([P, 1], F32, tag="quad_max", name="quad_max")
+            nc.vector.tensor_reduce(
+                out=neg[:], in_=turned_max[quad][:, 0:P], axis=AXIS.X, op=ALU.max, negate=True
+            )
+            quad_max[quad] = neg
+
+        def spread_maxima(quad):
+            spread = single_banks.tile([P, BANK], F32, tag="spread", name="spread_max")
             nc.tensor.transpose(
                 out=spread[:, 0:P],
-                in_=maxima[w][:, HALVES - 1 : HALVES].to_broadcast([P, P]),
+                in_=quad_max[quad][:, 0:1].to_broadcast([P, P]),
                 identity=ident[:],
             )
-            spreads[w] = spread
+            spread_max[quad] = spread
 
-        def step_maximum(w):
-            neg_max = small.tile([P, 1], F32, tag="neg_max")
-            nc.vector.tensor_reduce(
-                out=neg_max[:], in_=spreads[w][:, 0:P], axis=AXIS.X, op=ALU.max, negate=True
-            )
-            neg_maxes[w] = neg_max
+        def keep_maxima(quad):
+            neg = small.tile([P, GROUP], F32, tag="neg_max", name="neg_max")
+            nc.scalar.copy(out=neg[:], in_=spread_max[quad][:, 0:GROUP])
+            neg_maxes[quad] = neg
 
         def exponentials(w):
             e = e_tiles[w]
+            quad, column = quad_of[w]
             nc.scalar.activation(
-                out=e[:], in_=e[:], func=ACT.Exp, bias=neg_maxes[w][:, 0:1], scale=1.0
+                out=e[:],
+                in_=e[:],
+                func=ACT.Exp,
+                bias=neg_maxes[quad][:, column : column + 1],
+                scale=1.0,
             )
-            if w < STEPS - 1:
-                nc.gpsimd.tensor_tensor(out=den[:], in0=den[:], in1=e[:], op=ALU.add)
 
-        def products(w):
-            prod = prod_pool.tile([P, A], F32, tag="prod")
+        def add_to_denominator(w):
+            e = e_tiles[w]
+            if w >= STEPS - PE_ADDS:
+                return
             for h in range(HALVES):
-                cols = slice(h * BANK, (h + 1) * BANK)
-                nc.vector.tensor_tensor(
-                    out=prod[:, cols], in0=v_banks[w][h][:], in1=e_tiles[w][:, cols], op=ALU.mult
-                )
-            prod_tiles[w] = prod
+                if h == 1 or w < SPLIT_FROM:
+                    cols = slice(h * BANK, (h + 1) * BANK)
+                    nc.gpsimd.tensor_tensor(
+                        out=den[:, cols], in0=den[:, cols], in1=e[:, cols], op=ALU.add
+                    )
+
+        def products(w, h):
+            if h == 0:
+                prod_tiles[w] = prod_pool.tile([P, A], F32, tag="prod", name="prod")
+            cols = slice(h * BANK, (h + 1) * BANK)
+            nc.vector.tensor_tensor(
+                out=prod_tiles[w][:, cols],
+                in0=v_banks[w][h][:],
+                in1=e_tiles[w][:, cols],
+                op=ALU.mult,
+            )
 
         def add_transposed(bank, source, g, first, last):
             for t in range(PACK):
@@ -248,82 +347,129 @@ def tile_aftblock_pa_t_kernel(tc, z_current, z_window, Wq, Wk, Wv, Wo, out):
             for g in range(HALVES):
                 add_transposed(num_t[g], prod_tiles[w], g, w == 0, w == STEPS - 1)
 
-        gate_t = tail.tile([P, A], F32, name="gate_t")
-        rec_t = tail.tile([P, A], F32, name="rec_t")
+        q_exp = tail.tile([P, A], F32, name="q_exp")
+        gated_den = tail.tile([P, A], F32, name="gated_den")
+        root = tail.tile([P, A], F32, name="root")
         scale_t = tail.tile([P, A], F32, name="scale_t")
 
-        def gate():
-            for g in range(HALVES):
-                q_t = single_banks.tile([P, BANK], F32, tag=("turn", "spread")[g], name="q_t")
-                for t in range(PACK):
-                    c = g * PACK + t
-                    nc.tensor.matmul_mx(
-                        out=q_t[:, t * B : (t + 1) * B],
-                        lhsT=wq_codes[:, c * P : (c + 1) * P].bitcast(FP8X4),
-                        lhsT_scale=wq_scales[:, c * P : (c + 1) * P],
-                        rhs=zc_codes[:].bitcast(FP8X4),
-                        rhs_scale=zc_scales[:],
-                        start=True,
-                        stop=True,
-                    )
-                nc.scalar.activation(
-                    out=gate_t[:, g * BANK : (g + 1) * BANK], in_=q_t[:], func=ACT.Sigmoid
+        def gate(g):
+            q_t = single_banks.tile([P, BANK], F32, tag="spread", name="q_t")
+            for t in range(PACK):
+                c = g * PACK + t
+                nc.tensor.matmul_mx(
+                    out=q_t[:, t * B : (t + 1) * B],
+                    lhsT=wq_codes[:, c * P : (c + 1) * P].bitcast(FP8X4),
+                    lhsT_scale=wq_scales[:, c * P : (c + 1) * P],
+                    rhs=zc_codes[:].bitcast(FP8X4),
+                    rhs_scale=zc_scales[:],
+                    start=True,
+                    stop=True,
                 )
+            nc.scalar.activation(
+                out=q_exp[:, g * BANK : (g + 1) * BANK], in_=q_t[:], func=ACT.Exp, scale=-1.0
+            )
 
         den_t = {}
 
-        def turn_denominator():
-            for g in range(HALVES):
-                den_t[g] = key_banks.tile([P, BANK], F32, tag="keys", name="den_t")
-                add_transposed(den_t[g], den, g, True, False)
-                add_transposed(den_t[g], e_tiles[STEPS - 1], g, False, True)
+        def turn_denominator(source, g, last=False):
+            first = g not in den_t
+            if first:
+                den_t[g] = single_banks.tile([P, BANK], F32, tag=("turn", "spread")[g], name="den_t")
+            add_transposed(den_t[g], source, g, first, last)
 
-        def gate_over_denominator():
-            for g in range(HALVES):
-                cols = slice(g * BANK, (g + 1) * BANK)
-                nc.vector.reciprocal(out=rec_t[:, cols], in_=den_t[g][:])
-                nc.vector.tensor_tensor(
-                    out=scale_t[:, cols], in0=rec_t[:, cols], in1=gate_t[:, cols], op=ALU.mult
-                )
+        def gate_denominator(g):
+            cols = slice(g * BANK, (g + 1) * BANK)
+            nc.vector.scalar_tensor_tensor(
+                out=gated_den[:, cols],
+                in0=q_exp[:, cols],
+                scalar=1.0,
+                in1=den_t[g][:],
+                op0=ALU.add,
+                op1=ALU.mult,
+            )
 
-        value_grouped, later_grouped = {}, {}
-        for n in range(STEPS + LAG + 1):
+        def invert(g):
+            cols = slice(g * BANK, (g + 1) * BANK)
+            nc.scalar.activation(
+                out=root[:, cols], in_=gated_den[:, cols], func=ACT.Abs_reciprocal_sqrt
+            )
+            nc.scalar.activation(out=scale_t[:, cols], in_=root[:, cols], func=ACT.Square)
+
+        value_grouped, later_grouped, ordered = {}, {}, {}
+        for n in range(STEPS + LAG):
             j = n - LAG
-            if 2 <= n < STEPS + 2:
-                exponentials(n - 2)
+            quad = quad_end.get(n - 1)
+            spread_quad = quad_end.get(n - 2)
             if n < STEPS:
                 k_banks[n] = step_matmul(key_banks, "keys", n, wk_codes, wk_scales)
-            if n == STEPS + 1:
-                gate()
-            if 0 <= j < STEPS:
+            if 0 <= j <= STEPS - LAG:
                 v_banks[j] = step_matmul(value_banks, "values", j, wv_codes, wv_scales)
+            if STEPS <= n and j + 1 < STEPS:
+                banks, tag = ((key_banks, "keys"), (value_banks, "values"))[n % 2]
+                v_banks[j + 1] = step_matmul(banks, tag, j + 1, wv_codes, wv_scales)
+            if n in GATE_AT:
+                gate(GATE_AT.index(n))
             if n < STEPS:
                 park_keys(n, 0)
-            if 1 <= n <= len(value_groups):
-                quantise(value_groups[n - 1], value_grouped[n - 1])
+            if n in (2, 4):
+                quantise(value_weights[n // 2 - 1], value_grouped[n // 2 - 1])
             if 1 <= n <= len(stream) and stream[n - 1][2]:
                 quantise(later_groups[stream[n - 1][0]], later_grouped[stream[n - 1][0]])
-            if n < STEPS:
-                park_keys(n, 1)
-            if 1 <= n < STEPS + 1:
-                spread_maxima(n - 1)
-            if n == STEPS + 2:
-                turn_denominator()
-            if n < len(value_groups):
-                value_grouped[n] = turn_whole(value_groups[n])
+            if spread_quad is not None:
+                spread_maxima(spread_quad)
+                keep_maxima(spread_quad)
+            if n < len(value_stream):
+                index, half = value_stream[n]
+                if half == 0:
+                    value_grouped[index] = new_grouped()
+                turn_half(nc.scalar.copy, value_weights[index], value_grouped[index], half, value_banks, "values")
             if n < len(stream):
                 index, half = stream[n][0], stream[n][1]
                 if half == 0:
                     later_grouped[index] = new_grouped()
-                turn_half(later_groups[index], later_grouped[index], half, single_banks, "turn")
-            if 1 <= j < STEPS + 1:
+                turn_half(
+                    nc.scalar.copy,
+                    later_groups[index],
+                    later_grouped[index],
+                    half,
+                    single_banks,
+                    "turn",
+                    ordered.get(n),
+                )
+            if quad is not None:
+                turn_maxima(quad)
+            if 1 <= j:
                 sum_products(j - 1)
-            if 0 <= j < STEPS:
-                products(j)
-            if 1 <= n < STEPS + 1:
-                step_maximum(n - 1)
-            if n == STEPS + 2:
-                gate_over_denominator()
+            for w in exp_steps.get(n - 1, ()):
+                if w >= SPLIT_FROM:
+                    if w == SPLIT_FROM:
+                        turn_denominator(den, 0)
+                    turn_denominator(e_tiles[w], 0, w == STEPS - 1)
+            if n == STEPS + LAG - 3:
+                for w in range(STEPS - PE_ADDS, STEPS):
+                    turn_denominator(e_tiles[w], 1)
+                turn_denominator(den, 1, True)
+            if 0 <= j:
+                products(j, 0)
+            if n < STEPS:
+                park_keys(n, 1)
+            if quad is not None:
+                reduce_maxima(quad)
+            if n == STEPS + LAG - 2:
+                gate_denominator(0)
+                gate_denominator(1)
+                invert(0)
+                invert(1)
+            if 0 <= j:
+                products(j, 1)
+            for w in exp_steps.get(n, ()):
+                exponentials(w)
+                add_to_denominator(w)
+                if w == STEPS - 1:
+                    nc.scalar.activation(out=warm[:], in_=warm[:], func=ACT.Abs_reciprocal_sqrt)
+            if AHEAD <= n + AHEAD < len(stream):
+                ordered[n + AHEAD] = order_half(later_groups[stream[n + AHEAD][0]], stream[n + AHEAD][1])
+        sum_products(STEPS - 1)
 
         h_grouped = tail.tile([P, HALVES * B * PACK], BF16, name="h_grouped", align_bytes=64)
         h_codes = tail.tile([P, HALVES * B], U32, name="h_codes", align_bytes=64)
@@ -336,18 +482,30 @@ def tile_aftblock_pa_t_kernel(tc, z_current, z_window, Wq, Wk, Wv, Wo, out):
                 in1=scale_t[:, cols].rearrange("p (t b) -> p b t", t=PACK),
                 op=ALU.mult,
             )
-        nc.vector.quantize_mx(out=h_codes[:].bitcast(FP8X4), scales=h_scales[:], in_=h_grouped[:])
-        out_bank = single_banks.tile([P, BANK], F32, tag="turn")
         for g in range(HALVES):
-            nc.tensor.matmul_mx(
-                out=out_bank[:],
-                lhsT=h_codes[:, g * B : (g + 1) * B].bitcast(FP8X4),
-                lhsT_scale=h_scales[:, g * B : (g + 1) * B],
-                rhs=wo_codes[:, g * L : (g + 1) * L].bitcast(FP8X4),
-                rhs_scale=wo_scales[:, g * L : (g + 1) * L],
-                start=(g == 0),
-                stop=(g == HALVES - 1),
+            nc.vector.quantize_mx(
+                out=h_codes[:, g * B : (g + 1) * B].bitcast(FP8X4),
+                scales=h_scales[:, g * B : (g + 1) * B],
+                in_=h_grouped[:, g * BANK : (g + 1) * BANK],
             )
+        out_banks = [
+            value_banks.tile([P, BANK], F32, tag="values", name="out_bank") for i in range(2)
+        ]
+        half = L // 2
+        for i in range(2):
+            for g in range(HALVES):
+                cols = slice(g * L + i * half, g * L + (i + 1) * half)
+                nc.tensor.matmul_mx(
+                    out=out_banks[i][:, 0:half],
+                    lhsT=h_codes[:, g * B : (g + 1) * B].bitcast(FP8X4),
+                    lhsT_scale=h_scales[:, g * B : (g + 1) * B],
+                    rhs=wo_codes[:, cols].bitcast(FP8X4),
+                    rhs_scale=wo_scales[:, cols],
+                    start=(g == 0),
+                    stop=(g == HALVES - 1),
+                )
         result = tail.tile([P, L], F32, name="result")
-        nc.scalar.copy(out=result[:], in_=out_bank[:])
-        nc.sync.dma_start(out=out, in_=result[:])
+        nc.scalar.copy(out=result[:, 0:half], in_=out_banks[0][:, 0:half])
+        nc.scalar.dma_start(out=out[:, 0:half], in_=result[:, 0:half])
+        nc.vector.tensor_copy(out=result[:, half:L], in_=out_banks[1][:, 0:half])
+        nc.sync.dma_start(out=out[:, half:L], in_=result[:, half:L])

@@ -20,7 +20,7 @@ BANK = 512
 HALVES = A // BANK
 GROUP = 4
 LAG = 6
-PE_ADDS = 3
+PE_ADDS = 1
 QUADS = (2, 2, 4, 4, 4, 4, 4, 4, 2, 2)
 AHEAD = 2
 SPLIT_FROM = 20
@@ -189,6 +189,11 @@ def tile_aftblock_pa_t_kernel(tc, z_current, z_window, Wq, Wk, Wv, Wo, out):
                 nc.tensor.matmul(
                     out=num_t[0][:], lhsT=cold[:, 0:P], rhs=cold[:], start=True, stop=True
                 )
+
+        def fill(count):
+            bank = single_banks.tile([P, BANK], F32, tag="spread", name="filler")
+            for i in range(count):
+                nc.tensor.matmul(out=bank[:], lhsT=cold[:, 0:P], rhs=cold[:], start=True, stop=True)
 
         keep_warm(WARM)
         steps_groups = [steps_group(n) for n in range(STEPS // GROUP)]
@@ -440,6 +445,8 @@ def tile_aftblock_pa_t_kernel(tc, z_current, z_window, Wq, Wk, Wv, Wo, out):
                 turn_maxima(quad)
             if 1 <= j:
                 sum_products(j - 1)
+            if quad is None and LAG <= n < STEPS and 1 <= n <= len(stream) and stream[n - 1][2]:
+                fill(1)
             for w in exp_steps.get(n - 1, ()):
                 if w >= SPLIT_FROM:
                     if w == SPLIT_FROM:

@@ -24,6 +24,10 @@ PE_ADDS = 1
 QUADS = (2, 2, 4, 4, 4, 4, 4, 4, 2, 2)
 AHEAD = 2
 SPLIT_FROM = 20
+WHOLE_FROM = 20
+CH = 3
+DEN = 3
+DEN2 = 3
 WARM = 6
 HEADWARM = 0
 GATE_AT = (19, 23)
@@ -190,11 +194,6 @@ def tile_aftblock_pa_t_kernel(tc, z_current, z_window, Wq, Wk, Wv, Wo, out):
                     out=num_t[0][:], lhsT=cold[:, 0:P], rhs=cold[:], start=True, stop=True
                 )
 
-        def fill(count):
-            bank = single_banks.tile([P, BANK], F32, tag="spread", name="filler")
-            for i in range(count):
-                nc.tensor.matmul(out=bank[:], lhsT=cold[:, 0:P], rhs=cold[:], start=True, stop=True)
-
         keep_warm(WARM)
         steps_groups = [steps_group(n) for n in range(STEPS // GROUP)]
         key_weights = [weight_group(wk_raw, wk_codes, wk_scales, g) for g in range(2)]
@@ -228,6 +227,12 @@ def tile_aftblock_pa_t_kernel(tc, z_current, z_window, Wq, Wk, Wv, Wo, out):
             stream.extend([(index, half, half == pairs - 1) for half in range(pairs)])
         value_stream = [(g, half) for g in range(2) for half in range(2)]
 
+        def KD(n):
+            return 1 if n == 0 else 0
+
+        def VD(n):
+            return 0
+
         k_banks, v_banks, first_half_max, turned_max, quad_max, spread_max = {}, {}, {}, {}, {}, {}
         neg_maxes, e_tiles, prod_tiles = {}, {}, {}
 
@@ -241,12 +246,14 @@ def tile_aftblock_pa_t_kernel(tc, z_current, z_window, Wq, Wk, Wv, Wo, out):
             quad_end[first + size - 1] = quad
             first += size
 
-        def step_matmul(banks, tag, w, codes, scales):
+        def step_matmul(banks, tag, w, codes, scales, dummies=0):
             step = slice(w * B, (w + 1) * B)
             made = []
             for h in range(HALVES):
                 cols = slice(h * BANK, (h + 1) * BANK)
                 bank = banks.tile([P, BANK], F32, tag=tag, name="bank_" + tag)
+                if h < dummies:
+                    nc.tensor.matmul(out=bank[:], lhsT=cold[:, 0:P], rhs=cold[:], start=True, stop=True)
                 nc.tensor.matmul_mx(
                     out=bank[:],
                     lhsT=z_codes[:, step].bitcast(FP8X4),
@@ -318,12 +325,12 @@ def tile_aftblock_pa_t_kernel(tc, z_current, z_window, Wq, Wk, Wv, Wo, out):
             e = e_tiles[w]
             if w >= STEPS - PE_ADDS:
                 return
-            for h in range(HALVES):
-                if h == 1 or w < SPLIT_FROM:
-                    cols = slice(h * BANK, (h + 1) * BANK)
-                    nc.gpsimd.tensor_tensor(
-                        out=den[:, cols], in0=den[:, cols], in1=e[:, cols], op=ALU.add
-                    )
+            pieces = 2 if w < WHOLE_FROM else 1
+            low = CH * P if w >= SPLIT_FROM else 0
+            width = (A - low) // pieces
+            for i in range(pieces):
+                cols = slice(low + i * width, low + (i + 1) * width)
+                nc.gpsimd.tensor_tensor(out=den[:, cols], in0=den[:, cols], in1=e[:, cols], op=ALU.add)
 
         def products(w, h):
             if h == 0:
@@ -336,16 +343,16 @@ def tile_aftblock_pa_t_kernel(tc, z_current, z_window, Wq, Wk, Wv, Wo, out):
                 op=ALU.mult,
             )
 
-        def add_transposed(bank, source, g, first, last):
-            for t in range(PACK):
+        def add_transposed(bank, source, g, first, last, chunks=range(PACK)):
+            for t in chunks:
                 c = g * PACK + t
                 nc.tensor.matmul(
                     out=bank[:, t * B : (t + 1) * B],
                     lhsT=source[:, c * P : (c + 1) * P],
                     rhs=ident[:],
                     is_transpose=True,
-                    start=(first and t == 0),
-                    stop=(last and t == PACK - 1),
+                    start=(first and t == chunks[0]),
+                    stop=(last and t == chunks[-1]),
                 )
 
         def sum_products(w):
@@ -376,11 +383,11 @@ def tile_aftblock_pa_t_kernel(tc, z_current, z_window, Wq, Wk, Wv, Wo, out):
 
         den_t = {}
 
-        def turn_denominator(source, g, last=False):
+        def turn_denominator(source, g, chunks=range(PACK), last=False):
             first = g not in den_t
             if first:
                 den_t[g] = single_banks.tile([P, BANK], F32, tag=("turn", "spread")[g], name="den_t")
-            add_transposed(den_t[g], source, g, first, last)
+            add_transposed(den_t[g], source, g, first, last, chunks)
 
         def gate_denominator(g):
             cols = slice(g * BANK, (g + 1) * BANK)
@@ -406,12 +413,12 @@ def tile_aftblock_pa_t_kernel(tc, z_current, z_window, Wq, Wk, Wv, Wo, out):
             quad = quad_end.get(n - 1)
             spread_quad = quad_end.get(n - 2)
             if n < STEPS:
-                k_banks[n] = step_matmul(key_banks, "keys", n, wk_codes, wk_scales)
+                k_banks[n] = step_matmul(key_banks, "keys", n, wk_codes, wk_scales, KD(n))
             if 0 <= j <= STEPS - LAG:
-                v_banks[j] = step_matmul(value_banks, "values", j, wv_codes, wv_scales)
+                v_banks[j] = step_matmul(value_banks, "values", j, wv_codes, wv_scales, VD(n))
             if STEPS <= n and j + 1 < STEPS:
                 banks, tag = ((key_banks, "keys"), (value_banks, "values"))[n % 2]
-                v_banks[j + 1] = step_matmul(banks, tag, j + 1, wv_codes, wv_scales)
+                v_banks[j + 1] = step_matmul(banks, tag, j + 1, wv_codes, wv_scales, VD(n))
             if n in GATE_AT:
                 gate(GATE_AT.index(n))
             if n < STEPS:
@@ -445,17 +452,16 @@ def tile_aftblock_pa_t_kernel(tc, z_current, z_window, Wq, Wk, Wv, Wo, out):
                 turn_maxima(quad)
             if 1 <= j:
                 sum_products(j - 1)
-            if quad is None and LAG <= n < STEPS and 1 <= n <= len(stream) and stream[n - 1][2]:
-                fill(1)
             for w in exp_steps.get(n - 1, ()):
-                if w >= SPLIT_FROM:
-                    if w == SPLIT_FROM:
-                        turn_denominator(den, 0)
-                    turn_denominator(e_tiles[w], 0, w == STEPS - 1)
-            if n == STEPS + LAG - 3:
+                if SPLIT_FROM <= w < STEPS - PE_ADDS:
+                    turn_denominator(e_tiles[w], 0, range(CH))
+            if n == STEPS + DEN:
                 for w in range(STEPS - PE_ADDS, STEPS):
-                    turn_denominator(e_tiles[w], 1)
-                turn_denominator(den, 1, True)
+                    for g in range(HALVES):
+                        turn_denominator(e_tiles[w], g)
+            if n == STEPS + DEN2:
+                for g in range(HALVES):
+                    turn_denominator(den, g, range(PACK), True)
             if 0 <= j:
                 products(j, 0)
             if n < STEPS:

@@ -21,10 +21,10 @@ HALVES = A // BANK
 GROUP = 4
 LAG = 6
 PE_ADDS = 1
-QUADS = (2, 2, 4, 4, 4, 4, 4, 4, 2, 2)
+QUADS = (1, 3, 4, 4, 4, 4, 4, 4, 2, 2)
 AHEAD = 2
 SPLIT_FROM = 20
-WHOLE_FROM = 20
+WHOLE_FROM = 14
 CH = 3
 DEN = 3
 DEN2 = 3
@@ -228,7 +228,7 @@ def tile_aftblock_pa_t_kernel(tc, z_current, z_window, Wq, Wk, Wv, Wo, out):
         value_stream = [(g, half) for g in range(2) for half in range(2)]
 
         def KD(n):
-            return 1 if n == 0 else 0
+            return 2 if (n > LAG and n - 1 in set(i + 1 for i, s in enumerate(stream) if s[2])) else (1 if n == 0 else 0)
 
         def VD(n):
             return 0

@@ -131,18 +131,18 @@ def tile_aftblock_pa_t_kernel(tc, z_current, z_window, Wq, Wk, Wv, Wo, out):
         nc.sync.dma_start(out=zc_raw[:], in_=z_current)
         nc.sync.dma_start(out=wo_raw[:], in_=Wo.rearrange("(c p) a -> p c a", p=P))
 
-        z_codes = quant.tile([P, STEPS * B], U32, name="z_codes", align_bytes=64)
-        z_scales = quant.tile([P, STEPS * B], U8, name="z_scales", align_bytes=64)
-        zc_codes = quant.tile([P, B], U32, name="zc_codes", align_bytes=64)
-        zc_scales = quant.tile([P, B], U8, name="zc_scales", align_bytes=64)
-        wk_codes = quant.tile([P, A], U32, name="wk_codes", align_bytes=64)
-        wk_scales = quant.tile([P, A], U8, name="wk_scales", align_bytes=64)
-        wv_codes = quant.tile([P, A], U32, name="wv_codes", align_bytes=64)
-        wv_scales = quant.tile([P, A], U8, name="wv_scales", align_bytes=64)
-        wq_codes = quant.tile([P, A], U32, name="wq_codes", align_bytes=64)
-        wq_scales = quant.tile([P, A], U8, name="wq_scales", align_bytes=64)
-        wo_codes = quant.tile([P, 2 * L], U32, name="wo_codes", align_bytes=64)
-        wo_scales = quant.tile([P, 2 * L], U8, name="wo_scales", align_bytes=64)
+        z_codes = quant.tile([P, STEPS * B], U32, name="z_codes", align_bytes=256)
+        z_scales = quant.tile([P, STEPS * B], U8, name="z_scales", align_bytes=256)
+        zc_codes = quant.tile([P, B], U32, name="zc_codes", align_bytes=256)
+        zc_scales = quant.tile([P, B], U8, name="zc_scales", align_bytes=256)
+        wk_codes = quant.tile([P, A], U32, name="wk_codes", align_bytes=256)
+        wk_scales = quant.tile([P, A], U8, name="wk_scales", align_bytes=256)
+        wv_codes = quant.tile([P, A], U32, name="wv_codes", align_bytes=256)
+        wv_scales = quant.tile([P, A], U8, name="wv_scales", align_bytes=256)
+        wq_codes = quant.tile([P, A], U32, name="wq_codes", align_bytes=256)
+        wq_scales = quant.tile([P, A], U8, name="wq_scales", align_bytes=256)
+        wo_codes = quant.tile([P, 2 * L], U32, name="wo_codes", align_bytes=256)
+        wo_scales = quant.tile([P, 2 * L], U8, name="wo_scales", align_bytes=256)
 
         def weight_group(raw_tile, codes, scales, g):
             words = raw_tile[:].bitcast(F32)
@@ -468,13 +468,13 @@ def tile_aftblock_pa_t_kernel(tc, z_current, z_window, Wq, Wk, Wv, Wo, out):
                 park_keys(n, 1)
             if quad is not None:
                 reduce_maxima(quad)
+            if 0 <= j:
+                products(j, 1)
             if n == STEPS + LAG - 2:
                 gate_denominator(0)
                 gate_denominator(1)
                 invert(0)
                 invert(1)
-            if 0 <= j:
-                products(j, 1)
             for w in exp_steps.get(n, ()):
                 exponentials(w)
                 add_to_denominator(w)

from contextlib import ExitStack

import concourse.mybir as mybir
from concourse.masks import make_identity

F32 = mybir.dt.float32
BF16 = mybir.dt.bfloat16
U32 = mybir.dt.uint32
U8 = mybir.dt.uint8
FP8X4 = mybir.dt.float8_e4m3fn_x4
ACT = mybir.ActivationFunctionType
ALU = mybir.AluOpType
AXIS = mybir.AxisListType

P = 128
B, L, A, STEPS = 128, 512, 1024, 32
EPS = 1e-8
PACK = 4
BANK = 512
HALVES = A // BANK
GROUP = 4
LAG = 6
PE_ADDS = 1
QUADS = (1, 3, 4, 4, 4, 4, 4, 4, 2, 2)
AHEAD = 2
SPLIT_FROM = 20
WHOLE_FROM = 14
CH = 3
DEN = 3
DEN2 = 3
WARM = 6
HEADWARM = 0
GATE_AT = (19, 23)

FLOPS = 2 * B * L * A + 2 * 2 * STEPS * B * L * A + 2 * B * A * L


def order_pair(nc, pair, ordered):
    for r, words in enumerate(pair):
        nc.scalar.copy(
            out=ordered[:, r * 2 * P : (r + 1) * 2 * P].rearrange("p (u c) -> p u c", u=2),
            in_=words.rearrange("p (c u) -> p u c", u=2),
        )


def turn_pair(nc, copy, bank, ident, pair, ordered, grouped_words):
    for r, words in enumerate(pair):
        for u in range(2):
            if ordered is None:
                source = words[:, u : 2 * P : 2]
            else:
                source = ordered[:, (2 * r + u) * P : (2 * r + u + 1) * P]
            nc.tensor.transpose(
                out=bank[:, (2 * r + u) * P : (2 * r + u + 1) * P],
                in_=source,
                identity=ident[:],
            )
    width = len(pair) * 2 * P
    copy(
        out=grouped_words[:, 0:width].rearrange("p (r c u) -> p r c u", c=P, u=2),
        in_=bank[:, 0:width].rearrange("p (r u c) -> p r c u", u=2, c=P),
    )


def tile_aftblock_pa_t_kernel(tc, z_current, z_window, Wq, Wk, Wv, Wo, out):
    nc = tc.nc
    with ExitStack() as ctx:
        const = ctx.enter_context(tc.tile_pool(name="const", bufs=1))
        raw = ctx.enter_context(tc.tile_pool(name="raw", bufs=1))
        stage = ctx.enter_context(tc.tile_pool(name="stage", bufs=4))
        order_pool = ctx.enter_context(tc.tile_pool(name="order_pool", bufs=4))
        quant = ctx.enter_context(tc.tile_pool(name="quant", bufs=1))
        small = ctx.enter_context(tc.tile_pool(name="small", bufs=4))
        e_pool = ctx.enter_context(tc.tile_pool(name="e_pool", bufs=LAG + 4))
        prod_pool = ctx.enter_context(tc.tile_pool(name="prod_pool", bufs=3))
        tail = ctx.enter_context(tc.tile_pool(name="tail", bufs=1))
        sum_banks = ctx.enter_context(tc.psum_pool(name="sum_banks", bufs=1))
        key_banks = ctx.enter_context(tc.psum_pool(name="key_banks", bufs=2))
        value_banks = ctx.enter_context(tc.psum_pool(name="value_banks", bufs=2))
        single_banks = ctx.enter_context(tc.psum_pool(name="single_banks", bufs=1))

        ident = const.tile([P, P], F32, name="ident")
        make_identity(nc, ident[:])
        den = const.tile([P, A], F32, name="den")
        nc.vector.memset(den[:], EPS)
        row_maxima = [const.tile([P, P], F32, name="row_maxima%d" % i) for i in range(2)]
        for tile_of_maxima in row_maxima:
            nc.vector.memset(tile_of_maxima[:], 0.0)
        warm = const.tile([P, 1], F32, name="warm")
        nc.vector.memset(warm[:], 1.0)
        cold = const.tile([P, BANK], BF16, name="cold")
        nc.gpsimd.memset(cold[:], 0.0)

        ctx.enter_context(tc.manual_schedule())
        nc.scalar.activation(out=warm[:], in_=warm[:], func=ACT.Exp)

        wk_raw = raw.tile([P, HALVES, PACK * L], BF16, name="wk_raw")
        wv_raw = raw.tile([P, HALVES, PACK * L], BF16, name="wv_raw")
        wq_raw = raw.tile([P, HALVES, PACK * L], BF16, name="wq_raw")
        wo_raw = raw.tile([P, L // P, A], BF16, name="wo_raw")
        zc_raw = raw.tile([P, L], BF16, name="zc_raw")
        z_raw = [raw.tile([P, GROUP, L], BF16, name="z_raw%d" % n) for n in range(STEPS // GROUP)]

        def load_weight(tile_ap, weight, g, cols):
            nc.sync.dma_start(
                out=tile_ap[:, g, cols],
                in_=weight.rearrange("(g j t) l -> j g (t l)", g=HALVES, t=PACK)[:, g, cols],
            )

        def load_steps(n, first, last):
            nc.sync.dma_start(
                out=z_raw[n][:, first:last, :],
                in_=z_window[n * GROUP + first : n * GROUP + last].rearrange("w b l -> b w l"),
            )

        whole = slice(0, PACK * L)
        halves = (slice(0, 2 * L), slice(2 * L, 4 * L))
        load_weight(wk_raw, Wk, 0, halves[0])
        load_weight(wk_raw, Wk, 0, halves[1])
        load_steps(0, 0, 2)
        load_weight(wk_raw, Wk, 1, halves[0])
        load_weight(wk_raw, Wk, 1, halves[1])
        load_steps(0, 2, 4)
        load_weight(wv_raw, Wv, 0, whole)
        load_steps(1, 0, 4)
        load_weight(wv_raw, Wv, 1, whole)
        for n in range(2, STEPS // GROUP):
            load_steps(n, 0, 4)
        load_weight(wq_raw, Wq, 0, whole)
        load_weight(wq_raw, Wq, 1, whole)
        nc.sync.dma_start(out=zc_raw[:], in_=z_current)
        nc.sync.dma_start(out=wo_raw[:], in_=Wo.rearrange("(c p) a -> p c a", p=P))

        z_codes = quant.tile([P, STEPS * B], U32, name="z_codes", align_bytes=256)
        z_scales = quant.tile([P, STEPS * B], U8, name="z_scales", align_bytes=256)
        zc_codes = quant.tile([P, B], U32, name="zc_codes", align_bytes=256)
        zc_scales = quant.tile([P, B], U8, name="zc_scales", align_bytes=256)
        wk_codes = quant.tile([P, A], U32, name="wk_codes", align_bytes=256)
        wk_scales = quant.tile([P, A], U8, name="wk_scales", align_bytes=256)
        wv_codes = quant.tile([P, A], U32, name="wv_codes", align_bytes=256)
        wv_scales = quant.tile([P, A], U8, name="wv_scales", align_bytes=256)
        wq_codes = quant.tile([P, A], U32, name="wq_codes", align_bytes=256)
        wq_scales = quant.tile([P, A], U8, name="wq_scales", align_bytes=256)
        wo_codes = quant.tile([P, 2 * L], U32, name="wo_codes", align_bytes=256)
        wo_scales = quant.tile([P, 2 * L], U8, name="wo_scales", align_bytes=256)

        def weight_group(raw_tile, codes, scales, g):
            words = raw_tile[:].bitcast(F32)
            rows = [words[:, g, t * (L // 2) : (t + 1) * (L // 2)] for t in range(PACK)]
            cols = slice(g * BANK, (g + 1) * BANK)
            return (rows, codes[:, cols], scales[:, cols])

        def steps_group(n):
            words = z_raw[n][:].bitcast(F32)
            cols = slice(n * GROUP * B, (n + 1) * GROUP * B)
            return ([words[:, s, :] for s in range(GROUP)], z_codes[:, cols], z_scales[:, cols])

        def output_weight_group(g):
            words = wo_raw[:].bitcast(F32)
            rows = [words[:, c, g * (BANK // 2) : (g + 1) * (BANK // 2)] for c in range(L // P)]
            cols = slice(g * L, (g + 1) * L)
            return (rows, wo_codes[:, cols], wo_scales[:, cols])

        def half_group(group, half):
            cols = slice(2 * half * P, 2 * (half + 1) * P)
            return (group[0][2 * half : 2 * half + 2], group[1][:, cols], group[2][:, cols])

        def new_grouped():
            grouped = stage.tile([P, GROUP * P * PACK], BF16, tag="grouped", align_bytes=64)
            return grouped

        def order_half(group, half):
            ordered = order_pool.tile([P, BANK], F32, tag="ordered", name="ordered")
            order_pair(nc, group[0][2 * half : 2 * half + 2], ordered)
            return ordered

        def turn_half(copy, group, grouped, half, banks, tag, ordered=None):
            bank = banks.tile([P, BANK], F32, tag=tag, name="turned")
            words = grouped[:].bitcast(F32)[:, half * BANK : (half + 1) * BANK]
            turn_pair(nc, copy, bank, ident, group[0][2 * half : 2 * half + 2], ordered, words)

        def quantise(group, grouped):
            nc.vector.quantize_mx(
                out=group[1].bitcast(FP8X4),
                scales=group[2],
                in_=grouped[:, 0 : len(group[0]) * P * PACK],
            )

        num_t = [sum_banks.tile([P, BANK], F32, name="num_t%d" % g) for g in range(HALVES)]

        def keep_warm(count):
            for i in range(count):
                nc.tensor.matmul(
                    out=num_t[0][:], lhsT=cold[:, 0:P], rhs=cold[:], start=True, stop=True
                )

        keep_warm(WARM)
        steps_groups = [steps_group(n) for n in range(STEPS // GROUP)]
        key_weights = [weight_group(wk_raw, wk_codes, wk_scales, g) for g in range(2)]
        head = [
            (half_group(key_weights[0], 0), nc.scalar.copy, value_banks, "values"),
            (half_group(key_weights[0], 1), nc.vector.tensor_copy, value_banks, "values"),
            (half_group(steps_groups[0], 0), nc.scalar.copy, single_banks, "turn"),
            (half_group(key_weights[1], 0), nc.vector.tensor_copy, single_banks, "spread"),
            (half_group(key_weights[1], 1), nc.scalar.copy, value_banks, "values"),
        ]
        pending = []
        for group, copy, banks, tag in head:
            grouped = new_grouped()
            turn_half(copy, group, grouped, 0, banks, tag)
            keep_warm(HEADWARM)
            pending.append((group, grouped))
            if len(pending) > 1:
                quantise(*pending.pop(0))
        quantise(*pending.pop(0))
        value_weights = [weight_group(wv_raw, wv_codes, wv_scales, g) for g in range(2)]
        tail_groups = [weight_group(wq_raw, wq_codes, wq_scales, g) for g in range(2)]
        tail_groups.append(([zc_raw[:].bitcast(F32)], zc_codes[:], zc_scales[:]))
        tail_groups.extend([output_weight_group(g) for g in range(2)])
        later_groups = [half_group(steps_groups[0], 1)] + steps_groups[1:3]
        for i in range(5):
            later_groups.append(steps_groups[3 + i])
            later_groups.append(tail_groups[i])
        stream = []
        for index, group in enumerate(later_groups):
            pairs = (len(group[0]) + 1) // 2
            stream.extend([(index, half, half == pairs - 1) for half in range(pairs)])
        value_stream = [(g, half) for g in range(2) for half in range(2)]

        def KD(n):
            return 2 if (n > LAG and n - 1 in set(i + 1 for i, s in enumerate(stream) if s[2])) else (1 if n == 0 else 0)

        def VD(n):
            return 0

        k_banks, v_banks, first_half_max, turned_max, quad_max, spread_max = {}, {}, {}, {}, {}, {}
        neg_maxes, e_tiles, prod_tiles = {}, {}, {}

        quad_of, quad_end, exp_steps, exp_iteration = {}, {}, {}, {}
        first = 0
        for quad, size in enumerate(QUADS):
            for i in range(size):
                quad_of[first + i] = (quad, i)
                exp_iteration[first + i] = first + size + 1 + i
                exp_steps.setdefault(first + size + 1 + i, []).append(first + i)
            quad_end[first + size - 1] = quad
            first += size

        def step_matmul(banks, tag, w, codes, scales, dummies=0):
            step = slice(w * B, (w + 1) * B)
            made = []
            for h in range(HALVES):
                cols = slice(h * BANK, (h + 1) * BANK)
                bank = banks.tile([P, BANK], F32, tag=tag, name="bank_" + tag)
                if h < dummies:
                    nc.tensor.matmul(out=bank[:], lhsT=cold[:, 0:P], rhs=cold[:], start=True, stop=True)
                nc.tensor.matmul_mx(
                    out=bank[:],
                    lhsT=z_codes[:, step].bitcast(FP8X4),
                    lhsT_scale=z_scales[:, step],
                    rhs=codes[:, cols].bitcast(FP8X4),
                    rhs_scale=scales[:, cols],
                    start=True,
                    stop=True,
                )
                made.append(bank)
            return made

        def park_keys(w, h):
            if h == 0:
                e_tiles[w] = e_pool.tile([P, A], F32, tag="e", name="e")
                first_half_max[w] = small.tile([P, 1], F32, tag="first_half_max", name="first_half")
                accumulator = first_half_max[w][:, 0:1]
            else:
                quad, column = quad_of[w]
                accumulator = row_maxima[quad % 2][:, column : column + 1]
            nc.vector.tensor_scalar(
                out=e_tiles[w][:, h * BANK : (h + 1) * BANK],
                in0=k_banks[w][h][:],
                scalar1=1.0,
                scalar2=(None if h == 0 else first_half_max[w][:, 0:1]),
                op0=ALU.mult,
                op1=ALU.max,
                accum_out=accumulator,
            )

        def turn_maxima(quad):
            turned = single_banks.tile([P, BANK], F32, tag="spread", name="turned_max")
            nc.tensor.transpose(out=turned[:, 0:P], in_=row_maxima[quad % 2][:], identity=ident[:])
            turned_max[quad] = turned

        def reduce_maxima(quad):
            neg = small.tile([P, 1], F32, tag="quad_max", name="quad_max")
            nc.vector.tensor_reduce(
                out=neg[:], in_=turned_max[quad][:, 0:P], axis=AXIS.X, op=ALU.max, negate=True
            )
            quad_max[quad] = neg

        def spread_maxima(quad):
            spread = single_banks.tile([P, BANK], F32, tag="spread", name="spread_max")
            nc.tensor.transpose(
                out=spread[:, 0:P],
                in_=quad_max[quad][:, 0:1].to_broadcast([P, P]),
                identity=ident[:],
            )
            spread_max[quad] = spread

        def keep_maxima(quad):
            neg = small.tile([P, GROUP], F32, tag="neg_max", name="neg_max")
            nc.scalar.copy(out=neg[:], in_=spread_max[quad][:, 0:GROUP])
            neg_maxes[quad] = neg

        def exponentials(w):
            e = e_tiles[w]
            quad, column = quad_of[w]
            nc.scalar.activation(
                out=e[:],
                in_=e[:],
                func=ACT.Exp,
                bias=neg_maxes[quad][:, column : column + 1],
                scale=1.0,
            )

        def add_to_denominator(w):
            e = e_tiles[w]
            if w >= STEPS - PE_ADDS:
                return
            pieces = 2 if w < WHOLE_FROM else 1
            low = CH * P if w >= SPLIT_FROM else 0
            width = (A - low) // pieces
            for i in range(pieces):
                cols = slice(low + i * width, low + (i + 1) * width)
                nc.gpsimd.tensor_tensor(out=den[:, cols], in0=den[:, cols], in1=e[:, cols], op=ALU.add)

        def products(w, h):
            if h == 0:
                prod_tiles[w] = prod_pool.tile([P, A], F32, tag="prod", name="prod")
            cols = slice(h * BANK, (h + 1) * BANK)
            nc.vector.tensor_tensor(
                out=prod_tiles[w][:, cols],
                in0=v_banks[w][h][:],
                in1=e_tiles[w][:, cols],
                op=ALU.mult,
            )

        def add_transposed(bank, source, g, first, last, chunks=range(PACK)):
            for t in chunks:
                c = g * PACK + t
                nc.tensor.matmul(
                    out=bank[:, t * B : (t + 1) * B],
                    lhsT=source[:, c * P : (c + 1) * P],
                    rhs=ident[:],
                    is_transpose=True,
                    start=(first and t == chunks[0]),
                    stop=(last and t == chunks[-1]),
                )

        def sum_products(w):
            for g in range(HALVES):
                add_transposed(num_t[g], prod_tiles[w], g, w == 0, w == STEPS - 1)

        q_exp = tail.tile([P, A], F32, name="q_exp")
        gated_den = tail.tile([P, A], F32, name="gated_den")
        root = tail.tile([P, A], F32, name="root")
        scale_t = tail.tile([P, A], F32, name="scale_t")

        def gate(g):
            q_t = single_banks.tile([P, BANK], F32, tag="spread", name="q_t")
            for t in range(PACK):
                c = g * PACK + t
                nc.tensor.matmul_mx(
                    out=q_t[:, t * B : (t + 1) * B],
                    lhsT=wq_codes[:, c * P : (c + 1) * P].bitcast(FP8X4),
                    lhsT_scale=wq_scales[:, c * P : (c + 1) * P],
                    rhs=zc_codes[:].bitcast(FP8X4),
                    rhs_scale=zc_scales[:],
                    start=True,
                    stop=True,
                )
            nc.scalar.activation(
                out=q_exp[:, g * BANK : (g + 1) * BANK], in_=q_t[:], func=ACT.Exp, scale=-1.0
            )

        den_t = {}

        def turn_denominator(source, g, chunks=range(PACK), last=False):
            first = g not in den_t
            if first:
                den_t[g] = single_banks.tile([P, BANK], F32, tag=("turn", "spread")[g], name="den_t")
            add_transposed(den_t[g], source, g, first, last, chunks)

        def gate_denominator(g):
            cols = slice(g * BANK, (g + 1) * BANK)
            nc.vector.scalar_tensor_tensor(
                out=gated_den[:, cols],
                in0=q_exp[:, cols],
                scalar=1.0,
                in1=den_t[g][:],
                op0=ALU.add,
                op1=ALU.mult,
            )

        def invert(g):
            cols = slice(g * BANK, (g + 1) * BANK)
            nc.scalar.activation(
                out=root[:, cols], in_=gated_den[:, cols], func=ACT.Abs_reciprocal_sqrt
            )
            nc.scalar.activation(out=scale_t[:, cols], in_=root[:, cols], func=ACT.Square)

        value_grouped, later_grouped, ordered = {}, {}, {}
        for n in range(STEPS + LAG):
            j = n - LAG
            quad = quad_end.get(n - 1)
            spread_quad = quad_end.get(n - 2)
            if n < STEPS:
                k_banks[n] = step_matmul(key_banks, "keys", n, wk_codes, wk_scales, KD(n))
            if 0 <= j <= STEPS - LAG:
                v_banks[j] = step_matmul(value_banks, "values", j, wv_codes, wv_scales, VD(n))
            if STEPS <= n and j + 1 < STEPS:
                banks, tag = ((key_banks, "keys"), (value_banks, "values"))[n % 2]
                v_banks[j + 1] = step_matmul(banks, tag, j + 1, wv_codes, wv_scales, VD(n))
            if n in GATE_AT:
                gate(GATE_AT.index(n))
            if n < STEPS:
                park_keys(n, 0)
            if n in (2, 4):
                quantise(value_weights[n // 2 - 1], value_grouped[n // 2 - 1])
            if 1 <= n <= len(stream) and stream[n - 1][2]:
                quantise(later_groups[stream[n - 1][0]], later_grouped[stream[n - 1][0]])
            if spread_quad is not None:
                spread_maxima(spread_quad)
                keep_maxima(spread_quad)
            if n < len(value_stream):
                index, half = value_stream[n]
                if half == 0:
                    value_grouped[index] = new_grouped()
                turn_half(nc.scalar.copy, value_weights[index], value_grouped[index], half, value_banks, "values")
            if n < len(stream):
                index, half = stream[n][0], stream[n][1]
                if half == 0:
                    later_grouped[index] = new_grouped()
                turn_half(
                    nc.scalar.copy,
                    later_groups[index],
                    later_grouped[index],
                    half,
                    single_banks,
                    "turn",
                    ordered.get(n),
                )
            if quad is not None:
                turn_maxima(quad)
            if 1 <= j:
                sum_products(j - 1)
            for w in exp_steps.get(n - 1, ()):
                if SPLIT_FROM <= w < STEPS - PE_ADDS:
                    turn_denominator(e_tiles[w], 0, range(CH))
            if n == STEPS + DEN:
                for w in range(STEPS - PE_ADDS, STEPS):
                    for g in range(HALVES):
                        turn_denominator(e_tiles[w], g)
            if n == STEPS + DEN2:
                for g in range(HALVES):
                    turn_denominator(den, g, range(PACK), True)
            if 0 <= j:
                products(j, 0)
            if n < STEPS:
                park_keys(n, 1)
            if quad is not None:
                reduce_maxima(quad)
            if 0 <= j:
                products(j, 1)
            if n == STEPS + LAG - 2:
                gate_denominator(0)
                gate_denominator(1)
                invert(0)
                invert(1)
            for w in exp_steps.get(n, ()):
                exponentials(w)
                add_to_denominator(w)
                if w == STEPS - 1:
                    nc.scalar.activation(out=warm[:], in_=warm[:], func=ACT.Abs_reciprocal_sqrt)
            if AHEAD <= n + AHEAD < len(stream):
                ordered[n + AHEAD] = order_half(later_groups[stream[n + AHEAD][0]], stream[n + AHEAD][1])
        sum_products(STEPS - 1)

        h_grouped = tail.tile([P, HALVES * B * PACK], BF16, name="h_grouped", align_bytes=64)
        h_codes = tail.tile([P, HALVES * B], U32, name="h_codes", align_bytes=64)
        h_scales = tail.tile([P, HALVES * B], U8, name="h_scales", align_bytes=64)
        for g in range(HALVES):
            cols = slice(g * BANK, (g + 1) * BANK)
            nc.vector.tensor_tensor(
                out=h_grouped[:, cols].rearrange("p (b t) -> p b t", t=PACK),
                in0=num_t[g][:].rearrange("p (t b) -> p b t", t=PACK),
                in1=scale_t[:, cols].rearrange("p (t b) -> p b t", t=PACK),
                op=ALU.mult,
            )
        for g in range(HALVES):
            nc.vector.quantize_mx(
                out=h_codes[:, g * B : (g + 1) * B].bitcast(FP8X4),
                scales=h_scales[:, g * B : (g + 1) * B],
                in_=h_grouped[:, g * BANK : (g + 1) * BANK],
            )
        out_banks = [
            value_banks.tile([P, BANK], F32, tag="values", name="out_bank") for i in range(2)
        ]
        half = L // 2
        for i in range(2):
            for g in range(HALVES):
                cols = slice(g * L + i * half, g * L + (i + 1) * half)
                nc.tensor.matmul_mx(
                    out=out_banks[i][:, 0:half],
                    lhsT=h_codes[:, g * B : (g + 1) * B].bitcast(FP8X4),
                    lhsT_scale=h_scales[:, g * B : (g + 1) * B],
                    rhs=wo_codes[:, cols].bitcast(FP8X4),
                    rhs_scale=wo_scales[:, cols],
                    start=(g == 0),
                    stop=(g == HALVES - 1),
                )
        result = tail.tile([P, L], F32, name="result")
        nc.scalar.copy(out=result[:, 0:half], in_=out_banks[0][:, 0:half])
        nc.scalar.dma_start(out=out[:, 0:half], in_=result[:, 0:half])
        nc.vector.tensor_copy(out=result[:, half:L], in_=out_banks[1][:, 0:half])
        nc.sync.dma_start(out=out[:, half:L], in_=result[:, half:L])
